import numpy as np
import ml_dtypes


def mxq(x, axis, fmt="e4m3"):
    dtype, down = {"e4m3": (ml_dtypes.float8_e4m3fn, 7), "e5m2": (ml_dtypes.float8_e5m2, 14)}[fmt]
    v = np.moveaxis(np.asarray(x, np.float32).astype(ml_dtypes.bfloat16).astype(np.float64), axis, -1)
    blocks = v.reshape(v.shape[:-1] + (-1, 32))
    amax = np.abs(blocks).max(-1, keepdims=True)
    byte = np.maximum(np.where(amax > 0, np.frexp(amax)[1] - 1 + 127, 0) - down, 1)
    scale = np.exp2(byte - 127.0)
    codes = (blocks / scale).astype(np.float32).astype(dtype).astype(np.float64)
    return np.moveaxis((codes * scale).reshape(v.shape), -1, axis)


WIDE = False


def mx_kscale(k):
    if not WIDE:
        return np.ones(k)
    levels = np.array([10, -10, 5, -5, 0])
    if k % 512:
        return np.exp2(np.random.permutation(np.resize(levels, k // 32))).repeat(32)
    a = np.empty((k // 512, 16))
    for p in range(k // 512):
        a[p, :8] = np.random.permutation(np.resize(levels, 8))
        for g in range(8):
            far = levels[np.abs(levels - a[p, g]) >= 10]
            a[p, g + 8] = far[np.random.randint(len(far))]
    return np.exp2(a.ravel()).repeat(32)


BF16 = ml_dtypes.bfloat16


def bf(x):
    return np.asarray(x, np.float32).astype(BF16)


def f64(x):
    return np.asarray(x).astype(np.float64)


B, S, DIM, N_HEADS, Q_LORA, KV_LORA, NOPE, ROPE, V_HEAD = 4, 1024, 256, 2, 1536, 1024, 128, 64, 256
HV = N_HEADS * V_HEAD


def setup_inputs():
    s, t = mx_kscale(KV_LORA), mx_kscale(HV)
    return {"o_lat": bf(np.random.standard_normal((B, S, N_HEADS, KV_LORA)) * 0.35 * s),
            "w_uv": bf(np.random.standard_normal((N_HEADS, V_HEAD, KV_LORA)) * 2.0 / np.sqrt(KV_LORA) / s * t.reshape(N_HEADS, V_HEAD, 1)),
            "wo": bf(np.random.standard_normal((DIM, HV)) / np.sqrt(HV) / t)}


def reference(o_lat, w_uv, wo):
    ol = mxq(f64(o_lat), 3, "e4m3").transpose(0, 2, 1, 3)
    wv = mxq(f64(w_uv), 2, "e4m3").transpose(0, 2, 1)
    o = ol @ wv[None]
    o = o.transpose(0, 2, 1, 3).reshape(B, S, HV)
    return mxq(o, 2, "e4m3") @ mxq(f64(wo), 1, "e4m3").T

@@ -1,0 +1,229 @@
+from contextlib import ExitStack
+
+import concourse.masks as masks
+import concourse.mybir as mybir
+
+F32 = mybir.dt.float32
+BF16 = mybir.dt.bfloat16
+U32 = mybir.dt.uint32
+U8 = mybir.dt.uint8
+FP8X4 = mybir.dt.float8_e4m3fn_x4
+
+P = 128
+TOKENS = 4 * 1024
+HEADS = 2
+LATENT = 1024
+V_HEAD = 256
+JOINED = HEADS * V_HEAD
+DIM = 256
+PACK = 4
+PASSES = LATENT // (P * PACK)
+HEAD_WORDS = LATENT // 2
+PSUM_BANKS = 8
+TILES = TOKENS // P
+PAIRS = TILES // 2
+PAIRS_AHEAD = 8
+
+FLOPS = 2 * TOKENS * HEADS * V_HEAD * LATENT + 2 * TOKENS * JOINED * DIM
+
+
+def tile_mla_pc_t_kernel(tc, o_lat, w_uv, wo, out):
+    nc = tc.nc
+    x_rows = o_lat.rearrange("b (q t) h c -> (b q) t (h c)", t=TILES)
+    out_rows = out.rearrange("b (q t) f -> (b q) t f", t=TILES)
+
+    with ExitStack() as ctx:
+        keep = ctx.enter_context(tc.tile_pool(name="keep", bufs=1))
+        raw_pool = ctx.enter_context(tc.tile_pool(name="raw", bufs=PAIRS_AHEAD))
+        work = ctx.enter_context(tc.tile_pool(name="work", bufs=4))
+        banks = ctx.enter_context(tc.psum_pool(name="banks", bufs=PSUM_BANKS))
+        ctx.enter_context(tc.manual_schedule())
+
+        identity = keep.tile([P, P], F32)
+        masks.make_identity(nc, identity[:])
+
+        def transpose_row(words, first):
+            bank = banks.tile([P, HEAD_WORDS], F32, tag="bank")
+            for g in range(PASSES):
+                for u in range(2):
+                    block = 2 * g + u
+                    base = first + g * 2 * P
+                    nc.tensor.transpose(
+                        bank[:, block * P : (block + 1) * P],
+                        words[:, base + u : base + 2 * P : 2],
+                        identity[:],
+                    )
+            return bank
+
+        raw_of = {}
+        x_grouped_of = {}
+        x_quantised_of = {}
+        o_rounded_of = {}
+        o_grouped_of = {}
+        o_quantised_of = {}
+
+        def load(r):
+            if r < PAIRS:
+                raw = raw_pool.tile([P, 2 * HEADS * LATENT], BF16)
+                if r == 0:
+                    for i in range(2):
+                        nc.sync.dma_start(
+                            out=raw[:, i * HEADS * LATENT : (i + 1) * HEADS * LATENT],
+                            in_=x_rows[:, i, :],
+                        )
+                else:
+                    nc.sync.dma_start(
+                        out=raw[:].rearrange("p (i k) -> p i k", i=2),
+                        in_=x_rows[:, 2 * r : 2 * r + 2, :],
+                    )
+                raw_of[r] = raw
+
+        def transpose_x(r, i):
+            if r < PAIRS:
+                words = raw_of[r][:].bitcast(F32)
+                x_grouped = work.tile([P, HEADS * LATENT], BF16, align_bytes=64)
+                grouped_words = x_grouped[:].bitcast(F32)
+                for h in range(HEADS):
+                    bank = transpose_row(words, (i * HEADS + h) * HEAD_WORDS)
+                    nc.scalar.copy(
+                        out=grouped_words[:, h * HEAD_WORDS : (h + 1) * HEAD_WORDS].rearrange(
+                            "p (g r u) -> p g r u", g=PASSES, u=2
+                        ),
+                        in_=bank[:].rearrange("p (g u r) -> p g r u", g=PASSES, u=2),
+                    )
+                x_grouped_of[r, i] = x_grouped
+
+        def quantise_x(r, i):
+            if r < PAIRS:
+                x_codes = work.tile([P, HEADS * PASSES * P], U32, align_bytes=64)
+                x_scales = work.tile([P, HEADS * PASSES * P], U8, align_bytes=64)
+                nc.vector.quantize_mx(
+                    out=x_codes[:].bitcast(FP8X4), scales=x_scales[:], in_=x_grouped_of[r, i][:]
+                )
+                x_quantised_of[r, i] = (x_codes, x_scales)
+
+        def stage_1(r, i):
+            if 0 <= r < PAIRS:
+                x_codes, x_scales = x_quantised_of[r, i]
+                o_bank = banks.tile([P, JOINED], F32, tag="bank")
+                for h in range(HEADS):
+                    for g in range(PASSES):
+                        x_cols = slice((h * PASSES + g) * P, (h * PASSES + g + 1) * P)
+                        w_cols = slice((h * PASSES + g) * V_HEAD, (h * PASSES + g + 1) * V_HEAD)
+                        nc.tensor.matmul_mx(
+                            out=o_bank[:, h * V_HEAD : (h + 1) * V_HEAD],
+                            lhsT=x_codes[:, x_cols].bitcast(FP8X4),
+                            lhsT_scale=x_scales[:, x_cols],
+                            rhs=w_codes[:, w_cols].bitcast(FP8X4),
+                            rhs_scale=w_scales[:, w_cols],
+                            start=(g == 0),
+                            stop=(g == PASSES - 1),
+                        )
+                o_rounded = work.tile([P, JOINED], BF16)
+                nc.vector.tensor_copy(
+                    out=o_rounded[:].rearrange("p (u h n) -> p u h n", u=2, h=HEADS),
+                    in_=o_bank[:].rearrange("p (h u n) -> p u h n", u=2, h=HEADS),
+                )
+                o_rounded_of[r, i] = o_rounded
+
+        def transpose_o(r):
+            if 0 <= r < PAIRS:
+                bank = banks.tile([P, 2 * JOINED // 2], F32, tag="bank")
+                for i in range(2):
+                    words = o_rounded_of[r, i][:].bitcast(F32)
+                    for u in range(2):
+                        block = 2 * i + u
+                        nc.tensor.transpose(
+                            bank[:, block * P : (block + 1) * P],
+                            words[:, u * P : (u + 1) * P],
+                            identity[:],
+                        )
+                o_grouped = work.tile([P, 2 * JOINED], BF16, align_bytes=64)
+                nc.scalar.copy(
+                    out=o_grouped[:].bitcast(F32).rearrange("p (i r u) -> p i r u", i=2, u=2),
+                    in_=bank[:].rearrange("p (i u r) -> p i r u", i=2, u=2),
+                )
+                o_grouped_of[r] = o_grouped
+
+        def quantise_o(r):
+            if 0 <= r < PAIRS:
+                o_codes = work.tile([P, 2 * P], U32, align_bytes=64)
+                o_scales = work.tile([P, 2 * P], U8, align_bytes=64)
+                nc.vector.quantize_mx(
+                    out=o_codes[:].bitcast(FP8X4), scales=o_scales[:], in_=o_grouped_of[r][:]
+                )
+                o_quantised_of[r] = (o_codes, o_scales)
+
+        def stage_2(r):
+            if 0 <= r < PAIRS:
+                o_codes, o_scales = o_quantised_of[r]
+                out_bank = banks.tile([P, 2 * DIM], F32, tag="bank")
+                for i in range(2):
+                    nc.tensor.matmul_mx(
+                        out=out_bank[:, i * DIM : (i + 1) * DIM],
+                        lhsT=o_codes[:, i * P : (i + 1) * P].bitcast(FP8X4),
+                        lhsT_scale=o_scales[:, i * P : (i + 1) * P],
+                        rhs=wo_codes[:].bitcast(FP8X4),
+                        rhs_scale=wo_scales[:],
+                        start=True,
+                        stop=True,
+                    )
+                result = work.tile([P, 2 * DIM], F32)
+                nc.scalar.copy(out=result[:], in_=out_bank[:])
+                nc.sync.dma_start(
+                    out=out_rows[:, 2 * r : 2 * r + 2, :],
+                    in_=result[:].rearrange("p (i f) -> p i f", i=2),
+                )
+
+        w_raw = keep.tile([P, HEADS * 2 * LATENT], BF16)
+        w_rows = w_uv.rearrange("h (q e) c -> q h (e c)", e=2)
+        for h in range(HEADS):
+            nc.sync.dma_start(out=w_raw[:, h * 2 * LATENT : (h + 1) * 2 * LATENT], in_=w_rows[:, h, :])
+        wo_raw = keep.tile([P, 2 * JOINED], BF16)
+        nc.sync.dma_start(
+            out=wo_raw[:].rearrange("p (a k) -> p a k", a=DIM // P),
+            in_=wo.rearrange("(a p) k -> p a k", p=P),
+        )
+        for r in range(PAIRS_AHEAD):
+            load(r)
+
+        w_codes = keep.tile([P, HEADS * PASSES * V_HEAD], U32, align_bytes=64)
+        w_scales = keep.tile([P, HEADS * PASSES * V_HEAD], U8, align_bytes=64)
+        w_words = w_raw[:].bitcast(F32)
+        for h in range(HEADS):
+            w_grouped = work.tile([P, 2 * LATENT], BF16, align_bytes=64)
+            w_view = w_grouped[:].bitcast(F32).rearrange("p (g n v) -> p g n v", g=PASSES, v=2)
+            for u in range(2):
+                bank = transpose_row(w_words, (h * 2 + u) * HEAD_WORDS)
+                dst = w_view[:, :, u * P : (u + 1) * P, :]
+                src = bank[:].rearrange("p (g v r) -> p g r v", g=PASSES, v=2)
+                if u == 0:
+                    nc.scalar.copy(out=dst, in_=src)
+                else:
+                    nc.vector.tensor_copy(out=dst, in_=src)
+            cols = slice(h * PASSES * V_HEAD, (h + 1) * PASSES * V_HEAD)
+            nc.vector.quantize_mx(
+                out=w_codes[:, cols].bitcast(FP8X4), scales=w_scales[:, cols], in_=w_grouped[:]
+            )
+        wo_codes = keep.tile([P, DIM], U32, align_bytes=64)
+        wo_scales = keep.tile([P, DIM], U8, align_bytes=64)
+        wo_grouped = keep.tile([P, DIM * PACK], BF16, align_bytes=64)
+        wo_bank = transpose_row(wo_raw[:].bitcast(F32), 0)
+        for a in range(DIM // P):
+            nc.scalar.copy(
+                out=wo_grouped[:, a * P * PACK : (a + 1) * P * PACK].rearrange("p (r u e) -> p r u e", u=2, e=2),
+                in_=wo_bank[:, a * 2 * P : (a + 1) * 2 * P].bitcast(BF16).rearrange("p (e r u) -> p r u e", e=2, u=2),
+            )
+        nc.vector.quantize_mx(out=wo_codes[:].bitcast(FP8X4), scales=wo_scales[:], in_=wo_grouped[:])
+
+        for r in range(PAIRS + 2):
+            transpose_x(r, 0)
+            transpose_o(r - 2)
+            transpose_x(r, 1)
+            load(r + PAIRS_AHEAD)
+            quantise_x(r, 0)
+            quantise_o(r - 2)
+            stage_1(r - 1, 0)
+            stage_1(r - 1, 1)
+            stage_2(r - 2)
+            quantise_x(r, 1)

@@ -23,6 +23,9 @@ PSUM_BANKS = 8
 TILES = TOKENS // P
 PAIRS = TILES // 2
 PAIRS_AHEAD = 8
+ALL_PASSES = HEADS * PASSES
+SORTED = 2
+UNSORTED_PAIRS = 2
 
 FLOPS = 2 * TOKENS * HEADS * V_HEAD * LATENT + 2 * TOKENS * JOINED * DIM
 
@@ -42,20 +45,26 @@ def tile_mla_pc_t_kernel(tc, o_lat, w_uv, wo, out):
         identity = keep.tile([P, P], F32)
         masks.make_identity(nc, identity[:])
 
-        def transpose_row(words, first):
+        def copy(engine, out, in_):
+            if engine == "V":
+                nc.vector.tensor_copy(out=out, in_=in_)
+            else:
+                nc.scalar.copy(out=out, in_=in_)
+
+        def transpose_row(blocks):
             bank = banks.tile([P, HEAD_WORDS], F32, tag="bank")
-            for g in range(PASSES):
-                for u in range(2):
-                    block = 2 * g + u
-                    base = first + g * 2 * P
-                    nc.tensor.transpose(
-                        bank[:, block * P : (block + 1) * P],
-                        words[:, base + u : base + 2 * P : 2],
-                        identity[:],
-                    )
+            for n, block in enumerate(blocks):
+                nc.tensor.transpose(bank[:, n * P : (n + 1) * P], block, identity[:])
             return bank
 
+        def stepped(words, first):
+            return [words[:, first + u : first + 2 * P : 2] for u in range(2)]
+
+        def row_blocks(words, first):
+            return [b for g in range(PASSES) for b in stepped(words, first + g * 2 * P)]
+
         raw_of = {}
+        x_sorted_of = {}
         x_grouped_of = {}
         x_quantised_of = {}
         o_rounded_of = {}
@@ -65,11 +74,11 @@ def tile_mla_pc_t_kernel(tc, o_lat, w_uv, wo, out):
         def load(r):
             if r < PAIRS:
                 raw = raw_pool.tile([P, 2 * HEADS * LATENT], BF16)
-                if r == 0:
+                if r <= 2:
                     for i in range(2):
                         nc.sync.dma_start(
                             out=raw[:, i * HEADS * LATENT : (i + 1) * HEADS * LATENT],
-                            in_=x_rows[:, i, :],
+                            in_=x_rows[:, 2 * r + i, :],
                         )
                 else:
                     nc.sync.dma_start(
@@ -78,18 +87,40 @@ def tile_mla_pc_t_kernel(tc, o_lat, w_uv, wo, out):
                     )
                 raw_of[r] = raw
 
-        def transpose_x(r, i):
+        def sorted_passes(r):
+            return SORTED if UNSORTED_PAIRS <= r < PAIRS else 0
+
+        def sort_x(r, i):
+            count = sorted_passes(r)
+            if count:
+                x_sorted = work.tile([P, SORTED * 4 * P], BF16, align_bytes=64)
+                first = ((i + 1) * ALL_PASSES - count) * 2 * P
+                words = raw_of[r][:].bitcast(F32)[:, first : first + count * 2 * P]
+                nc.vector.tensor_copy(
+                    out=x_sorted[:].bitcast(F32).rearrange("p (n u r) -> p n u r", u=2, r=P),
+                    in_=words.rearrange("p (n r u) -> p n u r", u=2, r=P),
+                )
+                x_sorted_of[r, i] = x_sorted
+
+        def x_blocks(r, i, n):
+            skip = ALL_PASSES - sorted_passes(r)
+            if n < skip:
+                return stepped(raw_of[r][:].bitcast(F32), (i * ALL_PASSES + n) * 2 * P)
+            words = x_sorted_of[r, i][:].bitcast(F32)
+            return [words[:, (2 * (n - skip) + u) * P : (2 * (n - skip) + u + 1) * P] for u in range(2)]
+
+        def transpose_x(r, i, engines="SS"):
             if r < PAIRS:
-                words = raw_of[r][:].bitcast(F32)
                 x_grouped = work.tile([P, HEADS * LATENT], BF16, align_bytes=64)
                 grouped_words = x_grouped[:].bitcast(F32)
                 for h in range(HEADS):
-                    bank = transpose_row(words, (i * HEADS + h) * HEAD_WORDS)
-                    nc.scalar.copy(
-                        out=grouped_words[:, h * HEAD_WORDS : (h + 1) * HEAD_WORDS].rearrange(
+                    bank = transpose_row([b for g in range(PASSES) for b in x_blocks(r, i, h * PASSES + g)])
+                    copy(
+                        engines[h],
+                        grouped_words[:, h * HEAD_WORDS : (h + 1) * HEAD_WORDS].rearrange(
                             "p (g r u) -> p g r u", g=PASSES, u=2
                         ),
-                        in_=bank[:].rearrange("p (g u r) -> p g r u", g=PASSES, u=2),
+                        bank[:].rearrange("p (g u r) -> p g r u", g=PASSES, u=2),
                     )
                 x_grouped_of[r, i] = x_grouped
 
@@ -102,7 +133,7 @@ def tile_mla_pc_t_kernel(tc, o_lat, w_uv, wo, out):
                 )
                 x_quantised_of[r, i] = (x_codes, x_scales)
 
-        def stage_1(r, i):
+        def stage_1(r, i, engine="V"):
             if 0 <= r < PAIRS:
                 x_codes, x_scales = x_quantised_of[r, i]
                 o_bank = banks.tile([P, JOINED], F32, tag="bank")
@@ -120,71 +151,83 @@ def tile_mla_pc_t_kernel(tc, o_lat, w_uv, wo, out):
                             stop=(g == PASSES - 1),
                         )
                 o_rounded = work.tile([P, JOINED], BF16)
-                nc.vector.tensor_copy(
-                    out=o_rounded[:].rearrange("p (u h n) -> p u h n", u=2, h=HEADS),
-                    in_=o_bank[:].rearrange("p (h u n) -> p u h n", u=2, h=HEADS),
+                copy(
+                    engine,
+                    o_rounded[:].rearrange("p (u h n) -> p u h n", u=2, h=HEADS),
+                    o_bank[:].rearrange("p (h u n) -> p u h n", u=2, h=HEADS),
                 )
                 o_rounded_of[r, i] = o_rounded
 
-        def transpose_o(r):
-            if 0 <= r < PAIRS:
-                bank = banks.tile([P, 2 * JOINED // 2], F32, tag="bank")
-                for i in range(2):
-                    words = o_rounded_of[r, i][:].bitcast(F32)
+        def transpose_o(group, engine="S"):
+            if group:
+                n = len(group)
+                bank = banks.tile([P, n * JOINED // 2], F32, tag="bank")
+                for k, tile in enumerate(group):
+                    words = o_rounded_of[tile][:].bitcast(F32)
                     for u in range(2):
-                        block = 2 * i + u
+                        block = 2 * k + u
                         nc.tensor.transpose(
                             bank[:, block * P : (block + 1) * P],
                             words[:, u * P : (u + 1) * P],
                             identity[:],
                         )
-                o_grouped = work.tile([P, 2 * JOINED], BF16, align_bytes=64)
-                nc.scalar.copy(
-                    out=o_grouped[:].bitcast(F32).rearrange("p (i r u) -> p i r u", i=2, u=2),
-                    in_=bank[:].rearrange("p (i u r) -> p i r u", i=2, u=2),
+                o_grouped = work.tile([P, n * JOINED], BF16, align_bytes=64)
+                copy(
+                    engine,
+                    o_grouped[:].bitcast(F32).rearrange("p (i r u) -> p i r u", i=n, u=2),
+                    bank[:].rearrange("p (i u r) -> p i r u", i=n, u=2),
                 )
-                o_grouped_of[r] = o_grouped
+                o_grouped_of[group[0]] = o_grouped
 
-        def quantise_o(r):
-            if 0 <= r < PAIRS:
-                o_codes = work.tile([P, 2 * P], U32, align_bytes=64)
-                o_scales = work.tile([P, 2 * P], U8, align_bytes=64)
+        def quantise_o(group):
+            if group:
+                n = len(group)
+                o_codes = work.tile([P, n * P], U32, align_bytes=64)
+                o_scales = work.tile([P, n * P], U8, align_bytes=64)
                 nc.vector.quantize_mx(
-                    out=o_codes[:].bitcast(FP8X4), scales=o_scales[:], in_=o_grouped_of[r][:]
+                    out=o_codes[:].bitcast(FP8X4), scales=o_scales[:], in_=o_grouped_of[group[0]][:]
                 )
-                o_quantised_of[r] = (o_codes, o_scales)
+                o_quantised_of[group[0]] = (o_codes, o_scales)
 
-        def stage_2(r):
-            if 0 <= r < PAIRS:
-                o_codes, o_scales = o_quantised_of[r]
-                out_bank = banks.tile([P, 2 * DIM], F32, tag="bank")
-                for i in range(2):
+        def stage_2(group, engine="S"):
+            if group:
+                n = len(group)
+                o_codes, o_scales = o_quantised_of[group[0]]
+                out_bank = banks.tile([P, n * DIM], F32, tag="bank")
+                for k in range(n):
                     nc.tensor.matmul_mx(
-                        out=out_bank[:, i * DIM : (i + 1) * DIM],
-                        lhsT=o_codes[:, i * P : (i + 1) * P].bitcast(FP8X4),
-                        lhsT_scale=o_scales[:, i * P : (i + 1) * P],
+                        out=out_bank[:, k * DIM : (k + 1) * DIM],
+                        lhsT=o_codes[:, k * P : (k + 1) * P].bitcast(FP8X4),
+                        lhsT_scale=o_scales[:, k * P : (k + 1) * P],
                         rhs=wo_codes[:].bitcast(FP8X4),
                         rhs_scale=wo_scales[:],
                         start=True,
                         stop=True,
                     )
-                result = work.tile([P, 2 * DIM], F32)
-                nc.scalar.copy(out=result[:], in_=out_bank[:])
+                result = work.tile([P, n * DIM], F32)
+                copy(engine, result[:], out_bank[:])
+                t = 2 * group[0][0] + group[0][1]
                 nc.sync.dma_start(
-                    out=out_rows[:, 2 * r : 2 * r + 2, :],
-                    in_=result[:].rearrange("p (i f) -> p i f", i=2),
+                    out=out_rows[:, t : t + n, :],
+                    in_=result[:].rearrange("p (i f) -> p i f", i=n),
                 )
 
+        def pair(r):
+            return [(r, 0), (r, 1)] if 0 <= r < PAIRS else []
+
         w_raw = keep.tile([P, HEADS * 2 * LATENT], BF16)
-        w_rows = w_uv.rearrange("h (q e) c -> q h (e c)", e=2)
+        w_rows = w_uv.rearrange("h (q e) c -> q h e c", e=2)
         for h in range(HEADS):
-            nc.sync.dma_start(out=w_raw[:, h * 2 * LATENT : (h + 1) * 2 * LATENT], in_=w_rows[:, h, :])
+            for e in range(2):
+                n = 2 * h + e
+                nc.sync.dma_start(out=w_raw[:, n * LATENT : (n + 1) * LATENT], in_=w_rows[:, h, e, :])
+        load(0)
         wo_raw = keep.tile([P, 2 * JOINED], BF16)
         nc.sync.dma_start(
             out=wo_raw[:].rearrange("p (a k) -> p a k", a=DIM // P),
             in_=wo.rearrange("(a p) k -> p a k", p=P),
         )
-        for r in range(PAIRS_AHEAD):
+        for r in range(1, PAIRS_AHEAD):
             load(r)
 
         w_codes = keep.tile([P, HEADS * PASSES * V_HEAD], U32, align_bytes=64)
@@ -194,13 +237,12 @@ def tile_mla_pc_t_kernel(tc, o_lat, w_uv, wo, out):
             w_grouped = work.tile([P, 2 * LATENT], BF16, align_bytes=64)
             w_view = w_grouped[:].bitcast(F32).rearrange("p (g n v) -> p g n v", g=PASSES, v=2)
             for u in range(2):
-                bank = transpose_row(w_words, (h * 2 + u) * HEAD_WORDS)
-                dst = w_view[:, :, u * P : (u + 1) * P, :]
-                src = bank[:].rearrange("p (g v r) -> p g r v", g=PASSES, v=2)
-                if u == 0:
-                    nc.scalar.copy(out=dst, in_=src)
-                else:
-                    nc.vector.tensor_copy(out=dst, in_=src)
+                bank = transpose_row(row_blocks(w_words, (h * 2 + u) * HEAD_WORDS))
+                copy(
+                    "SV"[u],
+                    w_view[:, :, u * P : (u + 1) * P, :],
+                    bank[:].rearrange("p (g v r) -> p g r v", g=PASSES, v=2),
+                )
             cols = slice(h * PASSES * V_HEAD, (h + 1) * PASSES * V_HEAD)
             nc.vector.quantize_mx(
                 out=w_codes[:, cols].bitcast(FP8X4), scales=w_scales[:, cols], in_=w_grouped[:]
@@ -208,22 +250,41 @@ def tile_mla_pc_t_kernel(tc, o_lat, w_uv, wo, out):
         wo_codes = keep.tile([P, DIM], U32, align_bytes=64)
         wo_scales = keep.tile([P, DIM], U8, align_bytes=64)
         wo_grouped = keep.tile([P, DIM * PACK], BF16, align_bytes=64)
-        wo_bank = transpose_row(wo_raw[:].bitcast(F32), 0)
-        for a in range(DIM // P):
-            nc.scalar.copy(
-                out=wo_grouped[:, a * P * PACK : (a + 1) * P * PACK].rearrange("p (r u e) -> p r u e", u=2, e=2),
-                in_=wo_bank[:, a * 2 * P : (a + 1) * 2 * P].bitcast(BF16).rearrange("p (e r u) -> p r u e", e=2, u=2),
-            )
-        nc.vector.quantize_mx(out=wo_codes[:].bitcast(FP8X4), scales=wo_scales[:], in_=wo_grouped[:])
 
-        for r in range(PAIRS + 2):
+        def prepare_wo():
+            wo_bank = transpose_row(row_blocks(wo_raw[:].bitcast(F32), 0))
+            for a in range(DIM // P):
+                copy(
+                    "S",
+                    wo_grouped[:, a * P * PACK : (a + 1) * P * PACK].rearrange("p (r u e) -> p r u e", u=2, e=2),
+                    wo_bank[:, a * 2 * P : (a + 1) * 2 * P].bitcast(BF16).rearrange("p (e r u) -> p r u e", e=2, u=2),
+                )
+            nc.vector.quantize_mx(out=wo_codes[:].bitcast(FP8X4), scales=wo_scales[:], in_=wo_grouped[:])
+
+        for r in range(PAIRS):
             transpose_x(r, 0)
-            transpose_o(r - 2)
+            transpose_o(pair(r - 2))
             transpose_x(r, 1)
-            load(r + PAIRS_AHEAD)
+            if r == 1:
+                prepare_wo()
+            sort_x(r + 1, 0)
             quantise_x(r, 0)
-            quantise_o(r - 2)
+            quantise_o(pair(r - 2))
+            sort_x(r + 1, 1)
+            load(r + PAIRS_AHEAD)
             stage_1(r - 1, 0)
             stage_1(r - 1, 1)
-            stage_2(r - 2)
+            stage_2(pair(r - 2))
             quantise_x(r, 1)
+        last = PAIRS - 1
+        stage_1(last, 0)
+        transpose_o(pair(last - 1))
+        quantise_o(pair(last - 1))
+        stage_1(last, 1, "S")
+        stage_2(pair(last - 1))
+        for i in range(2):
+            transpose_o([(last, i)], "VS"[i])
+        for i in range(2):
+            quantise_o([(last, i)])
+        for i in range(2):
+            stage_2([(last, i)], "VS"[i])

@@ -24,8 +24,6 @@ TILES = TOKENS // P
 PAIRS = TILES // 2
 PAIRS_AHEAD = 8
 ALL_PASSES = HEADS * PASSES
-SORTED = 2
-UNSORTED_PAIRS = 2
 
 FLOPS = 2 * TOKENS * HEADS * V_HEAD * LATENT + 2 * TOKENS * JOINED * DIM
 
@@ -88,58 +86,65 @@ def tile_mla_pc_t_kernel(tc, o_lat, w_uv, wo, out):
                 raw_of[r] = raw
 
         def sorted_passes(r):
-            return SORTED if UNSORTED_PAIRS <= r < PAIRS else 0
+            return 8 if r >= 2 else 0
 
-        def sort_x(r, i):
-            count = sorted_passes(r)
-            if count:
-                x_sorted = work.tile([P, SORTED * 4 * P], BF16, align_bytes=64)
-                first = ((i + 1) * ALL_PASSES - count) * 2 * P
-                words = raw_of[r][:].bitcast(F32)[:, first : first + count * 2 * P]
+        def sort_x(r):
+            if r < PAIRS and sorted_passes(r):
+                count = sorted_passes(r) * P * PACK
+                x_sorted = work.tile([P, count], BF16, align_bytes=64, tag="x_sorted%d" % count)
+                words = raw_of[r][:, 2 * HEADS * LATENT - count :].bitcast(F32)
                 nc.vector.tensor_copy(
                     out=x_sorted[:].bitcast(F32).rearrange("p (n u r) -> p n u r", u=2, r=P),
                     in_=words.rearrange("p (n r u) -> p n u r", u=2, r=P),
                 )
-                x_sorted_of[r, i] = x_sorted
+                x_sorted_of[r] = x_sorted
 
         def x_blocks(r, i, n):
-            skip = ALL_PASSES - sorted_passes(r)
-            if n < skip:
-                return stepped(raw_of[r][:].bitcast(F32), (i * ALL_PASSES + n) * 2 * P)
-            words = x_sorted_of[r, i][:].bitcast(F32)
-            return [words[:, (2 * (n - skip) + u) * P : (2 * (n - skip) + u + 1) * P] for u in range(2)]
+            block = i * ALL_PASSES + n
+            skip = 2 * ALL_PASSES - sorted_passes(r)
+            if block >= skip:
+                words = x_sorted_of[r][:].bitcast(F32)
+                return [words[:, (2 * (block - skip) + u) * P : (2 * (block - skip) + u + 1) * P] for u in range(2)]
+            return stepped(raw_of[r][:].bitcast(F32), block * 2 * P)
 
         def transpose_x(r, i, engines="SS"):
             if r < PAIRS:
-                x_grouped = work.tile([P, HEADS * LATENT], BF16, align_bytes=64)
-                grouped_words = x_grouped[:].bitcast(F32)
+                if i == 0:
+                    x_grouped = work.tile([P, 2 * HEADS * LATENT], BF16, align_bytes=64)
+                    x_grouped_of[r] = x_grouped
+                grouped_words = x_grouped_of[r][:].bitcast(F32)
                 for h in range(HEADS):
                     bank = transpose_row([b for g in range(PASSES) for b in x_blocks(r, i, h * PASSES + g)])
                     copy(
                         engines[h],
-                        grouped_words[:, h * HEAD_WORDS : (h + 1) * HEAD_WORDS].rearrange(
+                        grouped_words[:, (i * HEADS + h) * HEAD_WORDS : (i * HEADS + h + 1) * HEAD_WORDS].rearrange(
                             "p (g r u) -> p g r u", g=PASSES, u=2
                         ),
                         bank[:].rearrange("p (g u r) -> p g r u", g=PASSES, u=2),
                     )
-                x_grouped_of[r, i] = x_grouped
 
-        def quantise_x(r, i):
-            if r < PAIRS:
-                x_codes = work.tile([P, HEADS * PASSES * P], U32, align_bytes=64)
-                x_scales = work.tile([P, HEADS * PASSES * P], U8, align_bytes=64)
-                nc.vector.quantize_mx(
-                    out=x_codes[:].bitcast(FP8X4), scales=x_scales[:], in_=x_grouped_of[r, i][:]
-                )
-                x_quantised_of[r, i] = (x_codes, x_scales)
+        def quantise_x(r, parts=1):
+            if 0 <= r < PAIRS:
+                x_codes = work.tile([P, 2 * HEADS * PASSES * P], U32, align_bytes=64)
+                x_scales = work.tile([P, 2 * HEADS * PASSES * P], U8, align_bytes=64)
+                width = 2 * HEADS * PASSES * P // parts
+                for n in range(parts):
+                    cols = slice(n * width, (n + 1) * width)
+                    nc.vector.quantize_mx(
+                        out=x_codes[:, cols].bitcast(FP8X4),
+                        scales=x_scales[:, cols],
+                        in_=x_grouped_of[r][:, n * width * PACK : (n + 1) * width * PACK],
+                    )
+                x_quantised_of[r] = (x_codes, x_scales)
 
         def stage_1(r, i, engine="V"):
             if 0 <= r < PAIRS:
-                x_codes, x_scales = x_quantised_of[r, i]
+                x_codes, x_scales = x_quantised_of[r]
                 o_bank = banks.tile([P, JOINED], F32, tag="bank")
                 for h in range(HEADS):
                     for g in range(PASSES):
-                        x_cols = slice((h * PASSES + g) * P, (h * PASSES + g + 1) * P)
+                        n = (i * HEADS + h) * PASSES + g
+                        x_cols = slice(n * P, (n + 1) * P)
                         w_cols = slice((h * PASSES + g) * V_HEAD, (h * PASSES + g + 1) * V_HEAD)
                         nc.tensor.matmul_mx(
                             out=o_bank[:, h * V_HEAD : (h + 1) * V_HEAD],
@@ -259,31 +264,34 @@ def tile_mla_pc_t_kernel(tc, o_lat, w_uv, wo, out):
                     wo_grouped[:, a * P * PACK : (a + 1) * P * PACK].rearrange("p (r u e) -> p r u e", u=2, e=2),
                     wo_bank[:, a * 2 * P : (a + 1) * 2 * P].bitcast(BF16).rearrange("p (e r u) -> p r u e", e=2, u=2),
                 )
-            nc.vector.quantize_mx(out=wo_codes[:].bitcast(FP8X4), scales=wo_scales[:], in_=wo_grouped[:])
 
+        def quantise_wo():
+            nc.vector.quantize_mx(out=wo_codes[:].bitcast(FP8X4), scales=wo_scales[:], in_=wo_grouped[:])
         for r in range(PAIRS):
+            if r == 2:
+                quantise_wo()
+            quantise_x(r - 1)
             transpose_x(r, 0)
-            transpose_o(pair(r - 2))
             transpose_x(r, 1)
             if r == 1:
                 prepare_wo()
-            sort_x(r + 1, 0)
-            quantise_x(r, 0)
-            quantise_o(pair(r - 2))
-            sort_x(r + 1, 1)
+            sort_x(r + 1)
             load(r + PAIRS_AHEAD)
-            stage_1(r - 1, 0)
-            stage_1(r - 1, 1)
-            stage_2(pair(r - 2))
-            quantise_x(r, 1)
+            transpose_o(pair(r - 2), "SS"[r % 2])
+            stage_2(pair(r - 3), "SS"[r % 2])
+            for i in range(2):
+                stage_1(r - 1, i)
+            quantise_o(pair(r - 2))
         last = PAIRS - 1
-        stage_1(last, 0)
-        transpose_o(pair(last - 1))
-        quantise_o(pair(last - 1))
+        quantise_x(last, parts=2)
+        transpose_o(pair(last - 1), "S")
+        stage_2(pair(last - 2), "S")
+        stage_1(last, 0, "V")
         stage_1(last, 1, "S")
-        stage_2(pair(last - 1))
+        quantise_o(pair(last - 1))
         for i in range(2):
             transpose_o([(last, i)], "VS"[i])
+        stage_2(pair(last - 1), "S")
         for i in range(2):
             quantise_o([(last, i)])
         for i in range(2):

@@ -23,6 +23,9 @@ PSUM_BANKS = 8
 TILES = TOKENS // P
 PAIRS = TILES // 2
 PAIRS_AHEAD = 8
+RUN = 2
+BY_HALF = (0, 2, 1, 3)
+AS_GIVEN = (0, 1, 2, 3)
 ALL_PASSES = HEADS * PASSES
 
 FLOPS = 2 * TOKENS * HEADS * V_HEAD * LATENT + 2 * TOKENS * JOINED * DIM
@@ -49,11 +52,18 @@ def tile_mla_pc_t_kernel(tc, o_lat, w_uv, wo, out):
             else:
                 nc.scalar.copy(out=out, in_=in_)
 
-        def transpose_row(blocks):
+        def transpose_row(blocks, order):
             bank = banks.tile([P, HEAD_WORDS], F32, tag="bank")
-            for n, block in enumerate(blocks):
+            for n, block in zip(order, blocks):
                 nc.tensor.transpose(bank[:, n * P : (n + 1) * P], block, identity[:])
             return bank
+
+        def interleave(engine, grouped_words, bank_words):
+            copy(
+                engine,
+                grouped_words.rearrange("p (c i u) -> p c u i", u=2, i=RUN),
+                bank_words.rearrange("p (u c i) -> p c u i", u=2, i=RUN),
+            )
 
         def stepped(words, first):
             return [words[:, first + u : first + 2 * P : 2] for u in range(2)]
@@ -86,7 +96,7 @@ def tile_mla_pc_t_kernel(tc, o_lat, w_uv, wo, out):
                 raw_of[r] = raw
 
         def sorted_passes(r):
-            return 8 if r >= 2 else 0
+            return 4 if r >= 2 else 0
 
         def sort_x(r):
             if r < PAIRS and sorted_passes(r):
@@ -114,14 +124,9 @@ def tile_mla_pc_t_kernel(tc, o_lat, w_uv, wo, out):
                     x_grouped_of[r] = x_grouped
                 grouped_words = x_grouped_of[r][:].bitcast(F32)
                 for h in range(HEADS):
-                    bank = transpose_row([b for g in range(PASSES) for b in x_blocks(r, i, h * PASSES + g)])
-                    copy(
-                        engines[h],
-                        grouped_words[:, (i * HEADS + h) * HEAD_WORDS : (i * HEADS + h + 1) * HEAD_WORDS].rearrange(
-                            "p (g r u) -> p g r u", g=PASSES, u=2
-                        ),
-                        bank[:].rearrange("p (g u r) -> p g r u", g=PASSES, u=2),
-                    )
+                    bank = transpose_row([b for g in range(PASSES) for b in x_blocks(r, i, h * PASSES + g)], BY_HALF)
+                    n = i * HEADS + h
+                    interleave(engines[h], grouped_words[:, n * HEAD_WORDS : (n + 1) * HEAD_WORDS], bank[:])
 
         def quantise_x(r, parts=1):
             if 0 <= r < PAIRS:
@@ -170,18 +175,14 @@ def tile_mla_pc_t_kernel(tc, o_lat, w_uv, wo, out):
                 for k, tile in enumerate(group):
                     words = o_rounded_of[tile][:].bitcast(F32)
                     for u in range(2):
-                        block = 2 * k + u
+                        block = n * u + k
                         nc.tensor.transpose(
                             bank[:, block * P : (block + 1) * P],
                             words[:, u * P : (u + 1) * P],
                             identity[:],
                         )
                 o_grouped = work.tile([P, n * JOINED], BF16, align_bytes=64)
-                copy(
-                    engine,
-                    o_grouped[:].bitcast(F32).rearrange("p (i r u) -> p i r u", i=n, u=2),
-                    bank[:].rearrange("p (i u r) -> p i r u", i=n, u=2),
-                )
+                interleave(engine, o_grouped[:].bitcast(F32), bank[:])
                 o_grouped_of[group[0]] = o_grouped
 
         def quantise_o(group):
@@ -242,7 +243,7 @@ def tile_mla_pc_t_kernel(tc, o_lat, w_uv, wo, out):
             w_grouped = work.tile([P, 2 * LATENT], BF16, align_bytes=64)
             w_view = w_grouped[:].bitcast(F32).rearrange("p (g n v) -> p g n v", g=PASSES, v=2)
             for u in range(2):
-                bank = transpose_row(row_blocks(w_words, (h * 2 + u) * HEAD_WORDS))
+                bank = transpose_row(row_blocks(w_words, (h * 2 + u) * HEAD_WORDS), AS_GIVEN)
                 copy(
                     "SV"[u],
                     w_view[:, :, u * P : (u + 1) * P, :],
@@ -257,7 +258,7 @@ def tile_mla_pc_t_kernel(tc, o_lat, w_uv, wo, out):
         wo_grouped = keep.tile([P, DIM * PACK], BF16, align_bytes=64)
 
         def prepare_wo():
-            wo_bank = transpose_row(row_blocks(wo_raw[:].bitcast(F32), 0))
+            wo_bank = transpose_row(row_blocks(wo_raw[:].bitcast(F32), 0), AS_GIVEN)
             for a in range(DIM // P):
                 copy(
                     "S",
@@ -277,7 +278,7 @@ def tile_mla_pc_t_kernel(tc, o_lat, w_uv, wo, out):
                 prepare_wo()
             sort_x(r + 1)
             load(r + PAIRS_AHEAD)
-            transpose_o(pair(r - 2), "SS"[r % 2])
+            transpose_o(pair(r - 2), "VV"[r % 2])
             stage_2(pair(r - 3), "SS"[r % 2])
             for i in range(2):
                 stage_1(r - 1, i)

@@ -40,6 +40,7 @@ def tile_mla_pc_t_kernel(tc, o_lat, w_uv, wo, out):
         keep = ctx.enter_context(tc.tile_pool(name="keep", bufs=1))
         raw_pool = ctx.enter_context(tc.tile_pool(name="raw", bufs=PAIRS_AHEAD))
         work = ctx.enter_context(tc.tile_pool(name="work", bufs=4))
+        deep = ctx.enter_context(tc.tile_pool(name="deep", bufs=8))
         banks = ctx.enter_context(tc.psum_pool(name="banks", bufs=PSUM_BANKS))
         ctx.enter_context(tc.manual_schedule())
 
@@ -96,7 +97,7 @@ def tile_mla_pc_t_kernel(tc, o_lat, w_uv, wo, out):
                 raw_of[r] = raw
 
         def sorted_passes(r):
-            return 4 if r >= 2 else 0
+            return 6 if r >= 2 else 0
 
         def sort_x(r):
             if r < PAIRS and sorted_passes(r):
@@ -119,36 +120,29 @@ def tile_mla_pc_t_kernel(tc, o_lat, w_uv, wo, out):
 
         def transpose_x(r, i, engines="SS"):
             if r < PAIRS:
-                if i == 0:
-                    x_grouped = work.tile([P, 2 * HEADS * LATENT], BF16, align_bytes=64)
-                    x_grouped_of[r] = x_grouped
-                grouped_words = x_grouped_of[r][:].bitcast(F32)
+                x_grouped = work.tile([P, HEADS * LATENT], BF16, align_bytes=64)
+                grouped_words = x_grouped[:].bitcast(F32)
                 for h in range(HEADS):
                     bank = transpose_row([b for g in range(PASSES) for b in x_blocks(r, i, h * PASSES + g)], BY_HALF)
-                    n = i * HEADS + h
-                    interleave(engines[h], grouped_words[:, n * HEAD_WORDS : (n + 1) * HEAD_WORDS], bank[:])
+                    interleave(engines[h], grouped_words[:, h * HEAD_WORDS : (h + 1) * HEAD_WORDS], bank[:])
+                x_grouped_of[r, i] = x_grouped
 
-        def quantise_x(r, parts=1):
+        def quantise_x(r, i):
             if 0 <= r < PAIRS:
-                x_codes = work.tile([P, 2 * HEADS * PASSES * P], U32, align_bytes=64)
-                x_scales = work.tile([P, 2 * HEADS * PASSES * P], U8, align_bytes=64)
-                width = 2 * HEADS * PASSES * P // parts
-                for n in range(parts):
-                    cols = slice(n * width, (n + 1) * width)
-                    nc.vector.quantize_mx(
-                        out=x_codes[:, cols].bitcast(FP8X4),
-                        scales=x_scales[:, cols],
-                        in_=x_grouped_of[r][:, n * width * PACK : (n + 1) * width * PACK],
-                    )
-                x_quantised_of[r] = (x_codes, x_scales)
+                x_codes = work.tile([P, HEADS * PASSES * P], U32, align_bytes=64)
+                x_scales = work.tile([P, HEADS * PASSES * P], U8, align_bytes=64)
+                nc.vector.quantize_mx(
+                    out=x_codes[:].bitcast(FP8X4), scales=x_scales[:], in_=x_grouped_of[r, i][:]
+                )
+                x_quantised_of[r, i] = (x_codes, x_scales)
 
         def stage_1(r, i, engine="V"):
             if 0 <= r < PAIRS:
-                x_codes, x_scales = x_quantised_of[r]
+                x_codes, x_scales = x_quantised_of[r, i]
                 o_bank = banks.tile([P, JOINED], F32, tag="bank")
                 for h in range(HEADS):
                     for g in range(PASSES):
-                        n = (i * HEADS + h) * PASSES + g
+                        n = h * PASSES + g
                         x_cols = slice(n * P, (n + 1) * P)
                         w_cols = slice((h * PASSES + g) * V_HEAD, (h * PASSES + g + 1) * V_HEAD)
                         nc.tensor.matmul_mx(
@@ -160,7 +154,7 @@ def tile_mla_pc_t_kernel(tc, o_lat, w_uv, wo, out):
                             start=(g == 0),
                             stop=(g == PASSES - 1),
                         )
-                o_rounded = work.tile([P, JOINED], BF16)
+                o_rounded = deep.tile([P, JOINED], BF16)
                 copy(
                     engine,
                     o_rounded[:].rearrange("p (u h n) -> p u h n", u=2, h=HEADS),
@@ -168,58 +162,65 @@ def tile_mla_pc_t_kernel(tc, o_lat, w_uv, wo, out):
                 )
                 o_rounded_of[r, i] = o_rounded
 
-        def transpose_o(group, engine="S"):
-            if group:
-                n = len(group)
-                bank = banks.tile([P, n * JOINED // 2], F32, tag="bank")
-                for k, tile in enumerate(group):
-                    words = o_rounded_of[tile][:].bitcast(F32)
-                    for u in range(2):
-                        block = n * u + k
-                        nc.tensor.transpose(
-                            bank[:, block * P : (block + 1) * P],
-                            words[:, u * P : (u + 1) * P],
-                            identity[:],
-                        )
-                o_grouped = work.tile([P, n * JOINED], BF16, align_bytes=64)
-                interleave(engine, o_grouped[:].bitcast(F32), bank[:])
-                o_grouped_of[group[0]] = o_grouped
+        o_bank_of = {}
+        out_bank_of = {}
 
-        def quantise_o(group):
-            if group:
-                n = len(group)
-                o_codes = work.tile([P, n * P], U32, align_bytes=64)
-                o_scales = work.tile([P, n * P], U8, align_bytes=64)
-                nc.vector.quantize_mx(
-                    out=o_codes[:].bitcast(FP8X4), scales=o_scales[:], in_=o_grouped_of[group[0]][:]
-                )
-                o_quantised_of[group[0]] = (o_codes, o_scales)
-
-        def stage_2(group, engine="S"):
-            if group:
-                n = len(group)
-                o_codes, o_scales = o_quantised_of[group[0]]
-                out_bank = banks.tile([P, n * DIM], F32, tag="bank")
-                for k in range(n):
-                    nc.tensor.matmul_mx(
-                        out=out_bank[:, k * DIM : (k + 1) * DIM],
-                        lhsT=o_codes[:, k * P : (k + 1) * P].bitcast(FP8X4),
-                        lhsT_scale=o_scales[:, k * P : (k + 1) * P],
-                        rhs=wo_codes[:].bitcast(FP8X4),
-                        rhs_scale=wo_scales[:],
-                        start=True,
-                        stop=True,
+        def transpose_o(r, i, engine="S", alone=False):
+            if 0 <= r < PAIRS:
+                n = 1 if alone else 2
+                k = 0 if alone else i
+                if k == 0:
+                    o_turned = banks.tile([P, n * JOINED // 2], F32, tag="bank")
+                    o_bank_of[r] = o_turned
+                words = o_rounded_of[r, i][:].bitcast(F32)
+                for u in range(2):
+                    block = n * u + k
+                    nc.tensor.transpose(
+                        o_bank_of[r][:, block * P : (block + 1) * P],
+                        words[:, u * P : (u + 1) * P],
+                        identity[:],
                     )
-                result = work.tile([P, n * DIM], F32)
-                copy(engine, result[:], out_bank[:])
-                t = 2 * group[0][0] + group[0][1]
-                nc.sync.dma_start(
-                    out=out_rows[:, t : t + n, :],
-                    in_=result[:].rearrange("p (i f) -> p i f", i=n),
-                )
+                if k == n - 1:
+                    o_grouped = work.tile([P, n * JOINED], BF16, align_bytes=64, tag="o_grouped%d" % n)
+                    interleave(engine, o_grouped[:].bitcast(F32), o_bank_of[r][:])
+                    o_grouped_of[r, i] = o_grouped
 
-        def pair(r):
-            return [(r, 0), (r, 1)] if 0 <= r < PAIRS else []
+        def quantise_o(r, alone=None):
+            if 0 <= r < PAIRS:
+                n = 2 if alone is None else 1
+                o_codes = work.tile([P, n * P], U32, align_bytes=64, tag="o_codes%d" % n)
+                o_scales = work.tile([P, n * P], U8, align_bytes=64, tag="o_scales%d" % n)
+                src = o_grouped_of[r, 1 if alone is None else alone]
+                nc.vector.quantize_mx(out=o_codes[:].bitcast(FP8X4), scales=o_scales[:], in_=src[:])
+                for i in range(2) if alone is None else [alone]:
+                    cols = slice(i * P, (i + 1) * P) if alone is None else slice(0, P)
+                    o_quantised_of[r, i] = (o_codes[:, cols], o_scales[:, cols])
+
+        def stage_2(r, i, engine="S", alone=False):
+            if 0 <= r < PAIRS:
+                n = 1 if alone else 2
+                k = 0 if alone else i
+                o_codes, o_scales = o_quantised_of[r, i]
+                if k == 0:
+                    out_bank = banks.tile([P, n * DIM], F32, tag="bank")
+                    out_bank_of[r] = out_bank
+                nc.tensor.matmul_mx(
+                    out=out_bank_of[r][:, k * DIM : (k + 1) * DIM],
+                    lhsT=o_codes.bitcast(FP8X4),
+                    lhsT_scale=o_scales,
+                    rhs=wo_codes[:].bitcast(FP8X4),
+                    rhs_scale=wo_scales[:],
+                    start=True,
+                    stop=True,
+                )
+                if k == n - 1:
+                    result = work.tile([P, n * DIM], F32, tag="result%d" % n)
+                    copy(engine, result[:], out_bank_of[r][:])
+                    t = 2 * r + i - n + 1
+                    nc.sync.dma_start(
+                        out=out_rows[:, t : t + n, :],
+                        in_=result[:].rearrange("p (i f) -> p i f", i=n),
+                    )
 
         w_raw = keep.tile([P, HEADS * 2 * LATENT], BF16)
         w_rows = w_uv.rearrange("h (q e) c -> q h e c", e=2)
@@ -268,32 +269,33 @@ def tile_mla_pc_t_kernel(tc, o_lat, w_uv, wo, out):
 
         def quantise_wo():
             nc.vector.quantize_mx(out=wo_codes[:].bitcast(FP8X4), scales=wo_scales[:], in_=wo_grouped[:])
-        for r in range(PAIRS):
+
+        for r in range(PAIRS + 1):
+            quantise_x(r - 1, 1)
             if r == 2:
                 quantise_wo()
-            quantise_x(r - 1)
+            quantise_o(r - 3)
+            sort_x(r + 1)
             transpose_x(r, 0)
+            transpose_o(r - 2, 0)
+            stage_1(r - 1, 0)
+            stage_2(r - 4, 1, "SS"[r % 2])
             transpose_x(r, 1)
+            quantise_x(r, 0)
             if r == 1:
                 prepare_wo()
-            sort_x(r + 1)
             load(r + PAIRS_AHEAD)
-            transpose_o(pair(r - 2), "VV"[r % 2])
-            stage_2(pair(r - 3), "SS"[r % 2])
-            for i in range(2):
-                stage_1(r - 1, i)
-            quantise_o(pair(r - 2))
+            transpose_o(r - 2, 1, "SS"[r % 2])
+            stage_1(r - 1, 1)
+            stage_2(r - 3, 0)
         last = PAIRS - 1
-        quantise_x(last, parts=2)
-        transpose_o(pair(last - 1), "S")
-        stage_2(pair(last - 2), "S")
-        stage_1(last, 0, "V")
-        stage_1(last, 1, "S")
-        quantise_o(pair(last - 1))
+        stage_2(last - 2, 1, "S")
+        quantise_o(last - 1)
+        transpose_o(last, 0, "V", alone=True)
+        transpose_o(last, 1, "S", alone=True)
+        stage_2(last - 1, 0)
+        stage_2(last - 1, 1, "S")
         for i in range(2):
-            transpose_o([(last, i)], "VS"[i])
-        stage_2(pair(last - 1), "S")
+            quantise_o(last, alone=i)
         for i in range(2):
-            quantise_o([(last, i)])
-        for i in range(2):
-            stage_2([(last, i)], "VS"[i])
+            stage_2(last, i, "VS"[i], alone=True)

@@ -24,6 +24,10 @@ TILES = TOKENS // P
 PAIRS = TILES // 2
 PAIRS_AHEAD = 8
 RUN = 2
+FIRST_SORTED = 3
+STEPPED = 2
+BY_POOL = 0
+BY_VECTOR = 6
 BY_HALF = (0, 2, 1, 3)
 AS_GIVEN = (0, 1, 2, 3)
 ALL_PASSES = HEADS * PASSES
@@ -74,6 +78,7 @@ def tile_mla_pc_t_kernel(tc, o_lat, w_uv, wo, out):
 
         raw_of = {}
         x_sorted_of = {}
+        x_by_pool_of = {}
         x_grouped_of = {}
         x_quantised_of = {}
         o_rounded_of = {}
@@ -96,27 +101,38 @@ def tile_mla_pc_t_kernel(tc, o_lat, w_uv, wo, out):
                     )
                 raw_of[r] = raw
 
-        def sorted_passes(r):
-            return 6 if r >= 2 else 0
+        def sort_passes(engine, r, first, count, dst):
+            src = raw_of[r][:].bitcast(U32)[:, first * 2 * P : (first + count) * 2 * P]
+            engine.tensor_copy(
+                out=dst.rearrange("p (n u r) -> p n u r", u=2, r=P),
+                in_=src.rearrange("p (n r u) -> p n u r", u=2, r=P),
+            )
 
-        def sort_x(r):
-            if r < PAIRS and sorted_passes(r):
-                count = sorted_passes(r) * P * PACK
-                x_sorted = work.tile([P, count], BF16, align_bytes=64, tag="x_sorted%d" % count)
-                words = raw_of[r][:, 2 * HEADS * LATENT - count :].bitcast(F32)
-                nc.vector.tensor_copy(
-                    out=x_sorted[:].bitcast(F32).rearrange("p (n u r) -> p n u r", u=2, r=P),
-                    in_=words.rearrange("p (n r u) -> p n u r", u=2, r=P),
-                )
-                x_sorted_of[r] = x_sorted
+        def sort_by_pool(r):
+            if FIRST_SORTED <= r < PAIRS and BY_POOL:
+                by_pool = work.tile([P, BY_POOL * 2 * P], U32)
+                for n in range(BY_POOL):
+                    cols = slice(n * 2 * P, (n + 1) * 2 * P)
+                    sort_passes(nc.gpsimd, r, STEPPED + n, 1, by_pool[:, cols])
+                x_by_pool_of[r] = by_pool
+
+        def sort_by_vector(r):
+            if FIRST_SORTED <= r < PAIRS:
+                by_vector = work.tile([P, BY_VECTOR * 2 * P], U32)
+                sort_passes(nc.vector, r, STEPPED + BY_POOL, BY_VECTOR, by_vector[:])
+                x_sorted_of[r] = by_vector
 
         def x_blocks(r, i, n):
             block = i * ALL_PASSES + n
-            skip = 2 * ALL_PASSES - sorted_passes(r)
-            if block >= skip:
+            if r < FIRST_SORTED or block < STEPPED:
+                return stepped(raw_of[r][:].bitcast(F32), block * 2 * P)
+            if block < STEPPED + BY_POOL:
+                words = x_by_pool_of[r][:].bitcast(F32)
+                block -= STEPPED
+            else:
                 words = x_sorted_of[r][:].bitcast(F32)
-                return [words[:, (2 * (block - skip) + u) * P : (2 * (block - skip) + u + 1) * P] for u in range(2)]
-            return stepped(raw_of[r][:].bitcast(F32), block * 2 * P)
+                block -= STEPPED + BY_POOL
+            return [words[:, (2 * block + u) * P : (2 * block + u + 1) * P] for u in range(2)]
 
         def transpose_x(r, i, engines="SS"):
             if r < PAIRS:
@@ -262,7 +278,7 @@ def tile_mla_pc_t_kernel(tc, o_lat, w_uv, wo, out):
             wo_bank = transpose_row(row_blocks(wo_raw[:].bitcast(F32), 0), AS_GIVEN)
             for a in range(DIM // P):
                 copy(
-                    "S",
+                    "VV"[a],
                     wo_grouped[:, a * P * PACK : (a + 1) * P * PACK].rearrange("p (r u e) -> p r u e", u=2, e=2),
                     wo_bank[:, a * 2 * P : (a + 1) * 2 * P].bitcast(BF16).rearrange("p (e r u) -> p r u e", e=2, u=2),
                 )
@@ -270,31 +286,39 @@ def tile_mla_pc_t_kernel(tc, o_lat, w_uv, wo, out):
         def quantise_wo():
             nc.vector.quantize_mx(out=wo_codes[:].bitcast(FP8X4), scales=wo_scales[:], in_=wo_grouped[:])
 
-        for r in range(PAIRS + 1):
+        last = PAIRS - 1
+        for r in range(PAIRS):
             quantise_x(r - 1, 1)
+            quantise_o(r - 3)
             if r == 2:
                 quantise_wo()
-            quantise_o(r - 3)
-            sort_x(r + 1)
             transpose_x(r, 0)
-            transpose_o(r - 2, 0)
             stage_1(r - 1, 0)
-            stage_2(r - 4, 1, "SS"[r % 2])
+            stage_2(r - 4, 1)
+            sort_by_vector(r + 1)
             transpose_x(r, 1)
             quantise_x(r, 0)
-            if r == 1:
+            if r == 0:
                 prepare_wo()
             load(r + PAIRS_AHEAD)
-            transpose_o(r - 2, 1, "SS"[r % 2])
+            transpose_o(r - 2, 0)
+            transpose_o(r - 2, 1)
             stage_1(r - 1, 1)
             stage_2(r - 3, 0)
-        last = PAIRS - 1
-        stage_2(last - 2, 1, "S")
+        quantise_x(last, 1)
+        quantise_o(last - 2)
+        transpose_o(last - 1, 0)
+        stage_1(last, 0)
+        stage_2(last - 3, 1)
+        transpose_o(last - 1, 1)
+        stage_1(last, 1)
+        stage_2(last - 2, 0)
+        stage_2(last - 2, 1)
         quantise_o(last - 1)
         transpose_o(last, 0, "V", alone=True)
         transpose_o(last, 1, "S", alone=True)
         stage_2(last - 1, 0)
-        stage_2(last - 1, 1, "S")
+        stage_2(last - 1, 1)
         for i in range(2):
             quantise_o(last, alone=i)
         for i in range(2):

@@ -23,7 +23,6 @@ PSUM_BANKS = 8
 TILES = TOKENS // P
 PAIRS = TILES // 2
 PAIRS_AHEAD = 8
-RUN = 2
 FIRST_SORTED = 3
 STEPPED = 2
 BY_POOL = 0
@@ -66,8 +65,8 @@ def tile_mla_pc_t_kernel(tc, o_lat, w_uv, wo, out):
         def interleave(engine, grouped_words, bank_words):
             copy(
                 engine,
-                grouped_words.rearrange("p (c i u) -> p c u i", u=2, i=RUN),
-                bank_words.rearrange("p (u c i) -> p c u i", u=2, i=RUN),
+                grouped_words.rearrange("p (n u) -> p n u", u=2),
+                bank_words.rearrange("p (u n) -> p n u", u=2),
             )
 
         def stepped(words, first):

from contextlib import ExitStack

import concourse.masks as masks
import concourse.mybir as mybir

F32 = mybir.dt.float32
BF16 = mybir.dt.bfloat16
U32 = mybir.dt.uint32
U8 = mybir.dt.uint8
FP8X4 = mybir.dt.float8_e4m3fn_x4

P = 128
TOKENS = 4 * 1024
HEADS = 2
LATENT = 1024
V_HEAD = 256
JOINED = HEADS * V_HEAD
DIM = 256
PACK = 4
PASSES = LATENT // (P * PACK)
HEAD_WORDS = LATENT // 2
PSUM_BANKS = 8
TILES = TOKENS // P
PAIRS = TILES // 2
PAIRS_AHEAD = 8
FIRST_SORTED = 3
STEPPED = 2
BY_POOL = 0
BY_VECTOR = 6
BY_HALF = (0, 2, 1, 3)
AS_GIVEN = (0, 1, 2, 3)
ALL_PASSES = HEADS * PASSES

FLOPS = 2 * TOKENS * HEADS * V_HEAD * LATENT + 2 * TOKENS * JOINED * DIM


def tile_mla_pc_t_kernel(tc, o_lat, w_uv, wo, out):
    nc = tc.nc
    x_rows = o_lat.rearrange("b (q t) h c -> (b q) t (h c)", t=TILES)
    out_rows = out.rearrange("b (q t) f -> (b q) t f", t=TILES)

    with ExitStack() as ctx:
        keep = ctx.enter_context(tc.tile_pool(name="keep", bufs=1))
        raw_pool = ctx.enter_context(tc.tile_pool(name="raw", bufs=PAIRS_AHEAD))
        work = ctx.enter_context(tc.tile_pool(name="work", bufs=4))
        deep = ctx.enter_context(tc.tile_pool(name="deep", bufs=8))
        banks = ctx.enter_context(tc.psum_pool(name="banks", bufs=PSUM_BANKS))
        ctx.enter_context(tc.manual_schedule())

        identity = keep.tile([P, P], F32)
        masks.make_identity(nc, identity[:])

        def copy(engine, out, in_):
            if engine == "V":
                nc.vector.tensor_copy(out=out, in_=in_)
            else:
                nc.scalar.copy(out=out, in_=in_)

        def transpose_row(blocks, order):
            bank = banks.tile([P, HEAD_WORDS], F32, tag="bank")
            for n, block in zip(order, blocks):
                nc.tensor.transpose(bank[:, n * P : (n + 1) * P], block, identity[:])
            return bank

        def interleave(engine, grouped_words, bank_words):
            copy(
                engine,
                grouped_words.rearrange("p (n u) -> p n u", u=2),
                bank_words.rearrange("p (u n) -> p n u", u=2),
            )

        def stepped(words, first):
            return [words[:, first + u : first + 2 * P : 2] for u in range(2)]

        def row_blocks(words, first):
            return [b for g in range(PASSES) for b in stepped(words, first + g * 2 * P)]

        raw_of = {}
        x_sorted_of = {}
        x_by_pool_of = {}
        x_grouped_of = {}
        x_quantised_of = {}
        o_rounded_of = {}
        o_grouped_of = {}
        o_quantised_of = {}

        def load(r):
            if r < PAIRS:
                raw = raw_pool.tile([P, 2 * HEADS * LATENT], BF16)
                if r <= 2:
                    for i in range(2):
                        nc.sync.dma_start(
                            out=raw[:, i * HEADS * LATENT : (i + 1) * HEADS * LATENT],
                            in_=x_rows[:, 2 * r + i, :],
                        )
                else:
                    nc.sync.dma_start(
                        out=raw[:].rearrange("p (i k) -> p i k", i=2),
                        in_=x_rows[:, 2 * r : 2 * r + 2, :],
                    )
                raw_of[r] = raw

        def sort_passes(engine, r, first, count, dst):
            src = raw_of[r][:].bitcast(U32)[:, first * 2 * P : (first + count) * 2 * P]
            engine.tensor_copy(
                out=dst.rearrange("p (n u r) -> p n u r", u=2, r=P),
                in_=src.rearrange("p (n r u) -> p n u r", u=2, r=P),
            )

        def sort_by_pool(r):
            if FIRST_SORTED <= r < PAIRS and BY_POOL:
                by_pool = work.tile([P, BY_POOL * 2 * P], U32)
                for n in range(BY_POOL):
                    cols = slice(n * 2 * P, (n + 1) * 2 * P)
                    sort_passes(nc.gpsimd, r, STEPPED + n, 1, by_pool[:, cols])
                x_by_pool_of[r] = by_pool

        def sort_by_vector(r):
            if FIRST_SORTED <= r < PAIRS:
                by_vector = work.tile([P, BY_VECTOR * 2 * P], U32)
                sort_passes(nc.vector, r, STEPPED + BY_POOL, BY_VECTOR, by_vector[:])
                x_sorted_of[r] = by_vector

        def x_blocks(r, i, n):
            block = i * ALL_PASSES + n
            if r < FIRST_SORTED or block < STEPPED:
                return stepped(raw_of[r][:].bitcast(F32), block * 2 * P)
            if block < STEPPED + BY_POOL:
                words = x_by_pool_of[r][:].bitcast(F32)
                block -= STEPPED
            else:
                words = x_sorted_of[r][:].bitcast(F32)
                block -= STEPPED + BY_POOL
            return [words[:, (2 * block + u) * P : (2 * block + u + 1) * P] for u in range(2)]

        def transpose_x(r, i, engines="SS"):
            if r < PAIRS:
                x_grouped = work.tile([P, HEADS * LATENT], BF16, align_bytes=64)
                grouped_words = x_grouped[:].bitcast(F32)
                for h in range(HEADS):
                    bank = transpose_row([b for g in range(PASSES) for b in x_blocks(r, i, h * PASSES + g)], BY_HALF)
                    interleave(engines[h], grouped_words[:, h * HEAD_WORDS : (h + 1) * HEAD_WORDS], bank[:])
                x_grouped_of[r, i] = x_grouped

        def quantise_x(r, i):
            if 0 <= r < PAIRS:
                x_codes = work.tile([P, HEADS * PASSES * P], U32, align_bytes=64)
                x_scales = work.tile([P, HEADS * PASSES * P], U8, align_bytes=64)
                nc.vector.quantize_mx(
                    out=x_codes[:].bitcast(FP8X4), scales=x_scales[:], in_=x_grouped_of[r, i][:]
                )
                x_quantised_of[r, i] = (x_codes, x_scales)

        def stage_1(r, i, engine="V"):
            if 0 <= r < PAIRS:
                x_codes, x_scales = x_quantised_of[r, i]
                o_bank = banks.tile([P, JOINED], F32, tag="bank")
                for h in range(HEADS):
                    for g in range(PASSES):
                        n = h * PASSES + g
                        x_cols = slice(n * P, (n + 1) * P)
                        w_cols = slice((h * PASSES + g) * V_HEAD, (h * PASSES + g + 1) * V_HEAD)
                        nc.tensor.matmul_mx(
                            out=o_bank[:, h * V_HEAD : (h + 1) * V_HEAD],
                            lhsT=x_codes[:, x_cols].bitcast(FP8X4),
                            lhsT_scale=x_scales[:, x_cols],
                            rhs=w_codes[:, w_cols].bitcast(FP8X4),
                            rhs_scale=w_scales[:, w_cols],
                            start=(g == 0),
                            stop=(g == PASSES - 1),
                        )
                o_rounded = deep.tile([P, JOINED], BF16)
                copy(
                    engine,
                    o_rounded[:].rearrange("p (u h n) -> p u h n", u=2, h=HEADS),
                    o_bank[:].rearrange("p (h u n) -> p u h n", u=2, h=HEADS),
                )
                o_rounded_of[r, i] = o_rounded

        o_bank_of = {}
        out_bank_of = {}

        def transpose_o(r, i, engine="S", alone=False):
            if 0 <= r < PAIRS:
                n = 1 if alone else 2
                k = 0 if alone else i
                if k == 0:
                    o_turned = banks.tile([P, n * JOINED // 2], F32, tag="bank")
                    o_bank_of[r] = o_turned
                words = o_rounded_of[r, i][:].bitcast(F32)
                for u in range(2):
                    block = n * u + k
                    nc.tensor.transpose(
                        o_bank_of[r][:, block * P : (block + 1) * P],
                        words[:, u * P : (u + 1) * P],
                        identity[:],
                    )
                if k == n - 1:
                    o_grouped = work.tile([P, n * JOINED], BF16, align_bytes=64, tag="o_grouped%d" % n)
                    interleave(engine, o_grouped[:].bitcast(F32), o_bank_of[r][:])
                    o_grouped_of[r, i] = o_grouped

        def quantise_o(r, alone=None):
            if 0 <= r < PAIRS:
                n = 2 if alone is None else 1
                o_codes = work.tile([P, n * P], U32, align_bytes=64, tag="o_codes%d" % n)
                o_scales = work.tile([P, n * P], U8, align_bytes=64, tag="o_scales%d" % n)
                src = o_grouped_of[r, 1 if alone is None else alone]
                nc.vector.quantize_mx(out=o_codes[:].bitcast(FP8X4), scales=o_scales[:], in_=src[:])
                for i in range(2) if alone is None else [alone]:
                    cols = slice(i * P, (i + 1) * P) if alone is None else slice(0, P)
                    o_quantised_of[r, i] = (o_codes[:, cols], o_scales[:, cols])

        def stage_2(r, i, engine="S", alone=False):
            if 0 <= r < PAIRS:
                n = 1 if alone else 2
                k = 0 if alone else i
                o_codes, o_scales = o_quantised_of[r, i]
                if k == 0:
                    out_bank = banks.tile([P, n * DIM], F32, tag="bank")
                    out_bank_of[r] = out_bank
                nc.tensor.matmul_mx(
                    out=out_bank_of[r][:, k * DIM : (k + 1) * DIM],
                    lhsT=o_codes.bitcast(FP8X4),
                    lhsT_scale=o_scales,
                    rhs=wo_codes[:].bitcast(FP8X4),
                    rhs_scale=wo_scales[:],
                    start=True,
                    stop=True,
                )
                if k == n - 1:
                    result = work.tile([P, n * DIM], F32, tag="result%d" % n)
                    copy(engine, result[:], out_bank_of[r][:])
                    t = 2 * r + i - n + 1
                    nc.sync.dma_start(
                        out=out_rows[:, t : t + n, :],
                        in_=result[:].rearrange("p (i f) -> p i f", i=n),
                    )

        w_raw = keep.tile([P, HEADS * 2 * LATENT], BF16)
        w_rows = w_uv.rearrange("h (q e) c -> q h e c", e=2)
        for h in range(HEADS):
            for e in range(2):
                n = 2 * h + e
                nc.sync.dma_start(out=w_raw[:, n * LATENT : (n + 1) * LATENT], in_=w_rows[:, h, e, :])
        load(0)
        wo_raw = keep.tile([P, 2 * JOINED], BF16)
        nc.sync.dma_start(
            out=wo_raw[:].rearrange("p (a k) -> p a k", a=DIM // P),
            in_=wo.rearrange("(a p) k -> p a k", p=P),
        )
        for r in range(1, PAIRS_AHEAD):
            load(r)

        w_codes = keep.tile([P, HEADS * PASSES * V_HEAD], U32, align_bytes=64)
        w_scales = keep.tile([P, HEADS * PASSES * V_HEAD], U8, align_bytes=64)
        w_words = w_raw[:].bitcast(F32)
        for h in range(HEADS):
            w_grouped = work.tile([P, 2 * LATENT], BF16, align_bytes=64)
            w_view = w_grouped[:].bitcast(F32).rearrange("p (g n v) -> p g n v", g=PASSES, v=2)
            for u in range(2):
                bank = transpose_row(row_blocks(w_words, (h * 2 + u) * HEAD_WORDS), AS_GIVEN)
                copy(
                    "SV"[u],
                    w_view[:, :, u * P : (u + 1) * P, :],
                    bank[:].rearrange("p (g v r) -> p g r v", g=PASSES, v=2),
                )
            cols = slice(h * PASSES * V_HEAD, (h + 1) * PASSES * V_HEAD)
            nc.vector.quantize_mx(
                out=w_codes[:, cols].bitcast(FP8X4), scales=w_scales[:, cols], in_=w_grouped[:]
            )
        wo_codes = keep.tile([P, DIM], U32, align_bytes=64)
        wo_scales = keep.tile([P, DIM], U8, align_bytes=64)
        wo_grouped = keep.tile([P, DIM * PACK], BF16, align_bytes=64)

        def prepare_wo():
            wo_bank = transpose_row(row_blocks(wo_raw[:].bitcast(F32), 0), AS_GIVEN)
            for a in range(DIM // P):
                copy(
                    "VV"[a],
                    wo_grouped[:, a * P * PACK : (a + 1) * P * PACK].rearrange("p (r u e) -> p r u e", u=2, e=2),
                    wo_bank[:, a * 2 * P : (a + 1) * 2 * P].bitcast(BF16).rearrange("p (e r u) -> p r u e", e=2, u=2),
                )

        def quantise_wo():
            nc.vector.quantize_mx(out=wo_codes[:].bitcast(FP8X4), scales=wo_scales[:], in_=wo_grouped[:])

        last = PAIRS - 1
        for r in range(PAIRS):
            quantise_x(r - 1, 1)
            quantise_o(r - 3)
            if r == 2:
                quantise_wo()
            transpose_x(r, 0)
            stage_1(r - 1, 0)
            stage_2(r - 4, 1)
            sort_by_vector(r + 1)
            transpose_x(r, 1)
            quantise_x(r, 0)
            if r == 0:
                prepare_wo()
            load(r + PAIRS_AHEAD)
            transpose_o(r - 2, 0)
            transpose_o(r - 2, 1)
            stage_1(r - 1, 1)
            stage_2(r - 3, 0)
        quantise_x(last, 1)
        quantise_o(last - 2)
        transpose_o(last - 1, 0)
        stage_1(last, 0)
        stage_2(last - 3, 1)
        transpose_o(last - 1, 1)
        stage_1(last, 1)
        stage_2(last - 2, 0)
        stage_2(last - 2, 1)
        quantise_o(last - 1)
        transpose_o(last, 0, "V", alone=True)
        transpose_o(last, 1, "S", alone=True)
        stage_2(last - 1, 0)
        stage_2(last - 1, 1)
        for i in range(2):
            quantise_o(last, alone=i)
        for i in range(2):
            stage_2(last, i, "VS"[i], alone=True)
